import numpy as np
import ml_dtypes


def mxq(x, axis, fmt="e4m3"):
    dtype, down = {"e4m3": (ml_dtypes.float8_e4m3fn, 7), "e5m2": (ml_dtypes.float8_e5m2, 14)}[fmt]
    v = np.moveaxis(np.asarray(x, np.float32).astype(ml_dtypes.bfloat16).astype(np.float64), axis, -1)
    blocks = v.reshape(v.shape[:-1] + (-1, 32))
    amax = np.abs(blocks).max(-1, keepdims=True)
    byte = np.maximum(np.where(amax > 0, np.frexp(amax)[1] - 1 + 127, 0) - down, 1)
    scale = np.exp2(byte - 127.0)
    codes = (blocks / scale).astype(np.float32).astype(dtype).astype(np.float64)
    return np.moveaxis((codes * scale).reshape(v.shape), -1, axis)


WIDE = False


def mx_kscale(k):
    if not WIDE:
        return np.ones(k)
    levels = np.array([10, -10, 5, -5, 0])
    a = np.random.permutation(np.resize(levels, k // 512 * 4)).reshape(k // 512, 4)
    idx = np.arange(k)
    return np.exp2(a[idx // 512, idx % 128 // 32])


BF16 = ml_dtypes.bfloat16


def bf(x):
    return np.asarray(x, np.float32).astype(BF16)


def f64(x):
    return np.asarray(x).astype(np.float64)


E2M1 = np.array([0.0, 0.5, 1.0, 1.5, 2.0, 3.0, 4.0, 6.0, -0.0, -0.5, -1.0, -1.5, -2.0, -3.0, -4.0, -6.0])


def pack_weight(w, fmt):
    k, n = w.shape
    w = f64(bf(w)).reshape(k // 32, 32, n)
    amax = np.abs(w).max(1)
    if fmt == "e4m3":
        byte = np.frexp(amax)[1] - 1 + 127 - 7
    else:
        mant, ex = np.frexp(amax / 6.0)
        byte = np.where(mant > 0.5, ex, ex - 1) + 127
    byte = np.clip(np.where(amax > 0, byte, 1), 1, 254)
    scaled = (w * np.exp2(127.0 - byte)[:, None, :]).reshape(k, n).astype(np.float32)
    by_word = np.ascontiguousarray(scaled.reshape(k // 512, 128, 4, n).transpose(0, 1, 3, 2))
    if fmt == "e4m3":
        words = by_word.astype(ml_dtypes.float8_e4m3fn).view(np.uint8)
    else:
        c = by_word.astype(ml_dtypes.float4_e2m1fn).view(np.uint8) & 0xF
        words = c[..., 0::2] | (c[..., 1::2] << 4)
    return np.ascontiguousarray(words), np.ascontiguousarray(byte.astype(np.uint8).reshape(k // 512, 16, n))


def unpack_weight(words, scales, fmt):
    g, p, n, _ = words.shape
    if fmt == "e4m3":
        vals = np.ascontiguousarray(words).view(ml_dtypes.float8_e4m3fn).astype(np.float64)
    else:
        nib = np.empty((g, p, n, 4), np.uint8)
        nib[..., 0::2] = words & 0xF
        nib[..., 1::2] = words >> 4
        vals = E2M1[nib]
    vals = vals * np.repeat(np.exp2(scales.astype(np.float64) - 127.0), 8, axis=1)[..., None]
    return vals.transpose(0, 1, 3, 2).reshape(g * 512, n)

def pack4(w):
    words, scales = pack_weight(w, "e2m1")
    return words.reshape(words.shape[0], 128, -1), scales


def unpack4(words, scales):
    return unpack_weight(words.reshape(words.shape[0], 128, -1, 2), scales, "e2m1")


B, N, R = 4096, 1024, 512


def setup_inputs():
    s = np.exp2(np.round(np.log2(mx_kscale(N)) / 2))
    input_state = bf(np.random.standard_normal((B, N)) * s)
    t = np.random.standard_normal((R, N)) * 0.03 / (s * s)[None, :]
    words, scales = pack4(np.ascontiguousarray(t.T))
    return {"input_state": input_state, "T_words": words, "T_scales": scales}


def reference(input_state, T_words, T_scales):
    x = f64(input_state)
    h = x * x
    return mxq(h, 1, "e4m3") @ unpack4(T_words, T_scales)

@@ -1,0 +1,140 @@
+from contextlib import ExitStack
+
+import concourse.mybir as mybir
+from concourse.masks import make_identity
+
+F32 = mybir.dt.float32
+BF16 = mybir.dt.bfloat16
+I32 = mybir.dt.int32
+U32 = mybir.dt.uint32
+U8 = mybir.dt.uint8
+FP8X4 = mybir.dt.float8_e4m3fn_x4
+FP4X4 = mybir.dt.float4_e2m1fn_x4
+SQUARE = mybir.ActivationFunctionType.Square
+
+P = 128
+B, K, R = 4096, 1024, 512
+TILES = B // P
+G = K // 512
+BUNCH = 4
+NB = TILES // BUNCH
+LOADS = [1, 1, 2, 4, 8, 8, 8]
+W_AFTER = 4
+
+FLOPS = 2 * B * K * R
+
+
+def tile_custom_final_pooling_2d_kernel(tc, input_state, T_words, T_scales, out):
+    nc = tc.nc
+    xv = input_state.rearrange("(p j) k -> p j k", j=TILES)
+    ov = out.rearrange("(p j) r -> p j r", j=TILES)
+    with ExitStack() as ctx:
+        const = ctx.enter_context(tc.tile_pool(name="const", bufs=1))
+        xpool = ctx.enter_context(tc.tile_pool(name="xpool", bufs=1))
+        gpool = ctx.enter_context(tc.tile_pool(name="gpool", bufs=6))
+        cpool = ctx.enter_context(tc.tile_pool(name="cpool", bufs=12))
+        opool = ctx.enter_context(tc.tile_pool(name="opool", bufs=4))
+        psum = ctx.enter_context(tc.psum_pool(name="psum", bufs=1))
+        ctx.enter_context(tc.manual_schedule())
+
+        w_sc = const.tile([P, G, R], U8, name="w_sc", align_bytes=64)
+        nc.vector.memset(w_sc[:].bitcast(I32), 0)
+        ident = const.tile([P, P], F32, name="ident")
+        make_identity(nc, ident[:])
+        w_words = const.tile([P, G, 2 * R], U8, name="w_words", align_bytes=64)
+
+        x_of = []
+        j0 = 0
+        for c, n in enumerate(LOADS):
+            if c == W_AFTER:
+                nc.sync.dma_start(
+                    out=w_words[:].bitcast(I32),
+                    in_=T_words.rearrange("g p b -> p g b").bitcast(I32),
+                )
+                for q in range(4):
+                    nc.sync.dma_start(
+                        out=w_sc[32 * q : 32 * q + 4, :, :].bitcast(I32),
+                        in_=T_scales.rearrange("g q n -> q g n")[4 * q : 4 * q + 4].bitcast(I32),
+                    )
+            xc = xpool.tile([P, n, K], BF16, name="x%d" % c)
+            nc.sync.dma_start(out=xc[:], in_=xv[:, j0 : j0 + n, :])
+            for i in range(n):
+                x_of.append(xc[:, i, :].bitcast(F32))
+            j0 += n
+
+        banks = {}
+        quant = {}
+        accs = {}
+        stage = {}
+
+        def transposes(j):
+            for i in range(BUNCH):
+                t = BUNCH * j + i
+                k = i if j == 0 else BUNCH + i
+                bank = psum.tile([P, 2, 256], F32, name="xt%d" % t, tag="bank%d" % k)
+                for g in range(G):
+                    for u in range(2):
+                        nc.tensor.transpose(
+                            bank[:, u, P * g : P * (g + 1)],
+                            x_of[t][:, 256 * g + u : 256 * (g + 1) : 2],
+                            ident[:],
+                        )
+                banks[t] = bank
+
+        def square(t):
+            grp = gpool.tile([P, K], BF16, name="grp%d" % t, tag="grp", align_bytes=64)
+            nc.scalar.activation(
+                out=grp[:].rearrange("p (w u e) -> p w u e", u=2, e=2),
+                in_=banks[t][:].bitcast(BF16).rearrange("p u (w e) -> p w u e", e=2),
+                func=SQUARE,
+            )
+            return grp
+
+        def quantise(t, grp):
+            codes = cpool.tile([P, K // 4], U32, name="codes%d" % t, tag="codes", align_bytes=64)
+            sc = cpool.tile([P, K // 4], U8, name="sc%d" % t, tag="sc", align_bytes=64)
+            nc.vector.quantize_mx(out=codes[:].bitcast(FP8X4), scales=sc[:], in_=grp[:])
+            quant[t] = (codes, sc)
+
+        def multiply(j):
+            for i in range(BUNCH):
+                t = BUNCH * j + i
+                codes, sc = quant[t]
+                acc = psum.tile([P, R], F32, name="acc%d" % t, tag="bank%d" % i)
+                for g in range(G):
+                    nc.tensor.matmul_mx(
+                        out=acc[:],
+                        lhsT=codes[:, P * g : P * (g + 1)].bitcast(FP8X4),
+                        lhsT_scale=sc[:, P * g : P * (g + 1)],
+                        rhs=w_words[:, g, :].bitcast(FP4X4),
+                        rhs_scale=w_sc[:, g, :],
+                        start=(g == 0),
+                        stop=(g == G - 1),
+                    )
+                accs[t] = acc
+
+        for j in range(NB + 1):
+            if j < NB:
+                transposes(j)
+            if j >= 1:
+                multiply(j - 1)
+                stage[j - 1] = opool.tile([P, BUNCH, R], F32, name="ost%d" % (j - 1), tag="ost")
+            for i in range(BUNCH):
+                if j < NB:
+                    t = BUNCH * j + i
+                    quantise(t, square(t))
+                if j >= 1:
+                    t = BUNCH * (j - 1) + i
+                    if j == NB and i % 2 == 1:
+                        nc.scalar.copy(out=stage[j - 1][:, i, :], in_=accs[t][:])
+                    else:
+                        nc.vector.tensor_copy(out=stage[j - 1][:, i, :], in_=accs[t][:])
+                    if j == NB and i >= 1:
+                        lo = 0 if i == 1 else i
+                        nc.sync.dma_start(
+                            out=ov[:, BUNCH * (j - 1) + lo : t + 1, :], in_=stage[j - 1][:, lo : i + 1, :]
+                        )
+            if 1 <= j < NB:
+                nc.sync.dma_start(
+                    out=ov[:, BUNCH * (j - 1) : BUNCH * j, :], in_=stage[j - 1][:]
+                )

@@ -20,6 +20,7 @@ BUNCH = 4
 NB = TILES // BUNCH
 LOADS = [1, 1, 2, 4, 8, 8, 8]
 W_AFTER = 4
+MULT = mybir.AluOpType.mult
 
 FLOPS = 2 * B * K * R
 
@@ -31,6 +32,7 @@ def tile_custom_final_pooling_2d_kernel(tc, input_state, T_words, T_scales, out)
     with ExitStack() as ctx:
         const = ctx.enter_context(tc.tile_pool(name="const", bufs=1))
         xpool = ctx.enter_context(tc.tile_pool(name="xpool", bufs=1))
+        hpool = ctx.enter_context(tc.tile_pool(name="hpool", bufs=6))
         gpool = ctx.enter_context(tc.tile_pool(name="gpool", bufs=6))
         cpool = ctx.enter_context(tc.tile_pool(name="cpool", bufs=12))
         opool = ctx.enter_context(tc.tile_pool(name="opool", bufs=4))
@@ -59,34 +61,46 @@ def tile_custom_final_pooling_2d_kernel(tc, input_state, T_words, T_scales, out)
             xc = xpool.tile([P, n, K], BF16, name="x%d" % c)
             nc.sync.dma_start(out=xc[:], in_=xv[:, j0 : j0 + n, :])
             for i in range(n):
-                x_of.append(xc[:, i, :].bitcast(F32))
+                x_of.append((xc, i))
             j0 += n
 
+        h_of = {}
         banks = {}
         quant = {}
         accs = {}
         stage = {}
+
+        def square(t, n):
+            xc, i = x_of[t]
+            hs = hpool.tile([P, 2, n * 512], BF16, name="hs%d" % t, tag="hs")
+            src = xc[:, i : i + n, :].rearrange("p n (w u e) -> p (n w) u e", u=2, e=2)
+            nc.vector.tensor_tensor(
+                out=hs[:].rearrange("p u (w e) -> p w u e", e=2), in0=src, in1=src, op=MULT
+            )
+            for d in range(n):
+                h_of[t + d] = (hs, d)
 
         def transposes(j):
             for i in range(BUNCH):
                 t = BUNCH * j + i
                 k = i if j == 0 else BUNCH + i
                 bank = psum.tile([P, 2, 256], F32, name="xt%d" % t, tag="bank%d" % k)
+                hs, d = h_of[t]
                 for g in range(G):
                     for u in range(2):
+                        lo = 256 * d + P * g
                         nc.tensor.transpose(
                             bank[:, u, P * g : P * (g + 1)],
-                            x_of[t][:, 256 * g + u : 256 * (g + 1) : 2],
+                            hs[:, u, :].bitcast(F32)[:, lo : lo + P],
                             ident[:],
                         )
                 banks[t] = bank
 
-        def square(t):
+        def regroup(t):
             grp = gpool.tile([P, K], BF16, name="grp%d" % t, tag="grp", align_bytes=64)
-            nc.scalar.activation(
-                out=grp[:].rearrange("p (w u e) -> p w u e", u=2, e=2),
-                in_=banks[t][:].bitcast(BF16).rearrange("p u (w e) -> p w u e", e=2),
-                func=SQUARE,
+            nc.scalar.copy(
+                out=grp[:].bitcast(F32).rearrange("p (w u) -> p w u", u=2),
+                in_=banks[t][:].rearrange("p u w -> p w u"),
             )
             return grp
 
@@ -113,28 +127,47 @@ def tile_custom_final_pooling_2d_kernel(tc, input_state, T_words, T_scales, out)
                     )
                 accs[t] = acc
 
+        def empty(t, on_vector):
+            dst = stage[t // BUNCH][:, t % BUNCH, :]
+            if on_vector:
+                nc.vector.tensor_copy(out=dst, in_=accs[t][:])
+            else:
+                nc.scalar.copy(out=dst, in_=accs[t][:])
+
+        square(0, 1)
+        square(1, 1)
+        square(2, 2)
         for j in range(NB + 1):
+            a = BUNCH * j
+            o = a - BUNCH
             if j < NB:
                 transposes(j)
             if j >= 1:
                 multiply(j - 1)
                 stage[j - 1] = opool.tile([P, BUNCH, R], F32, name="ost%d" % (j - 1), tag="ost")
-            for i in range(BUNCH):
-                if j < NB:
-                    t = BUNCH * j + i
-                    quantise(t, square(t))
+            if j + 1 < NB:
+                square(a + 4, 2)
+            if j < NB:
+                quantise(a, regroup(a))
+                quantise(a + 1, regroup(a + 1))
+            if j + 1 < NB:
+                square(a + 6, 2)
+            if j < NB:
+                g2 = regroup(a + 2)
                 if j >= 1:
-                    t = BUNCH * (j - 1) + i
-                    if j == NB and i % 2 == 1:
-                        nc.scalar.copy(out=stage[j - 1][:, i, :], in_=accs[t][:])
-                    else:
-                        nc.vector.tensor_copy(out=stage[j - 1][:, i, :], in_=accs[t][:])
-                    if j == NB and i >= 1:
-                        lo = 0 if i == 1 else i
-                        nc.sync.dma_start(
-                            out=ov[:, BUNCH * (j - 1) + lo : t + 1, :], in_=stage[j - 1][:, lo : i + 1, :]
-                        )
-            if 1 <= j < NB:
-                nc.sync.dma_start(
-                    out=ov[:, BUNCH * (j - 1) : BUNCH * j, :], in_=stage[j - 1][:]
-                )
+                    empty(o, False)
+                quantise(a + 2, g2)
+                quantise(a + 3, regroup(a + 3))
+                if j >= 1:
+                    empty(o + 1, False)
+                    empty(o + 2, False)
+                    empty(o + 3, True)
+                    nc.sync.dma_start(out=ov[:, o : o + BUNCH, :], in_=stage[j - 1][:])
+            else:
+                empty(o, True)
+                empty(o + 1, False)
+                nc.sync.dma_start(out=ov[:, o : o + 2, :], in_=stage[j - 1][:, 0:2, :])
+                empty(o + 2, True)
+                nc.sync.dma_start(out=ov[:, o + 2 : o + 3, :], in_=stage[j - 1][:, 2:3, :])
+                empty(o + 3, False)
+                nc.sync.dma_start(out=ov[:, o + 3 : o + 4, :], in_=stage[j - 1][:, 3:4, :])

@@ -73,9 +73,9 @@ def tile_custom_final_pooling_2d_kernel(tc, input_state, T_words, T_scales, out)
         def square(t, n):
             xc, i = x_of[t]
             hs = hpool.tile([P, 2, n * 512], BF16, name="hs%d" % t, tag="hs")
-            src = xc[:, i : i + n, :].rearrange("p n (w u e) -> p (n w) u e", u=2, e=2)
+            src = xc[:, i : i + n, :].rearrange("p n (w u e) -> p u (n w) e", u=2, e=2)
             nc.vector.tensor_tensor(
-                out=hs[:].rearrange("p u (w e) -> p w u e", e=2), in0=src, in1=src, op=MULT
+                out=hs[:].rearrange("p u (w e) -> p u w e", e=2), in0=src, in1=src, op=MULT
             )
             for d in range(n):
                 h_of[t + d] = (hs, d)

@@ -16,13 +16,27 @@ P = 128
 B, K, R = 4096, 1024, 512
 TILES = B // P
 G = K // 512
-BUNCH = 4
+BUNCH = 2
 NB = TILES // BUNCH
+LAG = 2
 LOADS = [1, 1, 2, 4, 8, 8, 8]
-W_AFTER = 4
+W_AFTER = 2
+WARM = 6
 MULT = mybir.AluOpType.mult
 
 FLOPS = 2 * B * K * R
+
+
+def is_sorted(t):
+    return t >= 4 and t % 2 == 1
+
+
+def empties_on_vector(t):
+    return t % 8 in (0, 2, 3, 5, 6)
+
+
+def store_size(t):
+    return 4 if t < 24 else 2
 
 
 def tile_custom_final_pooling_2d_kernel(tc, input_state, T_words, T_scales, out):
@@ -39,6 +53,8 @@ def tile_custom_final_pooling_2d_kernel(tc, input_state, T_words, T_scales, out)
         psum = ctx.enter_context(tc.psum_pool(name="psum", bufs=1))
         ctx.enter_context(tc.manual_schedule())
 
+        zeros = const.tile([P, 512], BF16, name="zeros")
+        nc.vector.memset(zeros[:], 0.0)
         w_sc = const.tile([P, G, R], U8, name="w_sc", align_bytes=64)
         nc.vector.memset(w_sc[:].bitcast(I32), 0)
         ident = const.tile([P, P], F32, name="ident")
@@ -61,7 +77,7 @@ def tile_custom_final_pooling_2d_kernel(tc, input_state, T_words, T_scales, out)
             xc = xpool.tile([P, n, K], BF16, name="x%d" % c)
             nc.sync.dma_start(out=xc[:], in_=xv[:, j0 : j0 + n, :])
             for i in range(n):
-                x_of.append((xc, i))
+                x_of.append(xc[:, i, :])
             j0 += n
 
         h_of = {}
@@ -70,38 +86,47 @@ def tile_custom_final_pooling_2d_kernel(tc, input_state, T_words, T_scales, out)
         accs = {}
         stage = {}
 
-        def square(t, n):
-            xc, i = x_of[t]
-            hs = hpool.tile([P, 2, n * 512], BF16, name="hs%d" % t, tag="hs")
-            src = xc[:, i : i + n, :].rearrange("p n (w u e) -> p u (n w) e", u=2, e=2)
-            nc.vector.tensor_tensor(
-                out=hs[:].rearrange("p u (w e) -> p u w e", e=2), in0=src, in1=src, op=MULT
-            )
+        idle = psum.tile([P, 512], F32, name="idle", tag="bank7")
+
+        def dummies(n):
             for d in range(n):
-                h_of[t + d] = (hs, d)
+                nc.tensor.matmul(out=idle[:], lhsT=zeros[:, 0:P], rhs=zeros[:], start=True, stop=True)
+
+        def square_sorted(t):
+            hs = hpool.tile([P, 2, 512], BF16, name="hs%d" % t, tag="hs")
+            src = x_of[t].rearrange("p (w u e) -> p w u e", u=2, e=2)
+            nc.vector.tensor_tensor(
+                out=hs[:].rearrange("p u (w e) -> p w u e", e=2), in0=src, in1=src, op=MULT
+            )
+            h_of[t] = hs
 
         def transposes(j):
             for i in range(BUNCH):
                 t = BUNCH * j + i
-                k = i if j == 0 else BUNCH + i
+                k = BUNCH * j + i if j < 2 else 4 + BUNCH * (j % 2) + i
                 bank = psum.tile([P, 2, 256], F32, name="xt%d" % t, tag="bank%d" % k)
-                hs, d = h_of[t]
                 for g in range(G):
                     for u in range(2):
-                        lo = 256 * d + P * g
-                        nc.tensor.transpose(
-                            bank[:, u, P * g : P * (g + 1)],
-                            hs[:, u, :].bitcast(F32)[:, lo : lo + P],
-                            ident[:],
-                        )
+                        if is_sorted(t):
+                            src = h_of[t][:, u, :].bitcast(F32)[:, P * g : P * (g + 1)]
+                        else:
+                            src = x_of[t].bitcast(F32)[:, 256 * g + u : 256 * (g + 1) : 2]
+                        nc.tensor.transpose(bank[:, u, P * g : P * (g + 1)], src, ident[:])
                 banks[t] = bank
 
         def regroup(t):
             grp = gpool.tile([P, K], BF16, name="grp%d" % t, tag="grp", align_bytes=64)
-            nc.scalar.copy(
-                out=grp[:].bitcast(F32).rearrange("p (w u) -> p w u", u=2),
-                in_=banks[t][:].rearrange("p u w -> p w u"),
-            )
+            if is_sorted(t):
+                nc.scalar.copy(
+                    out=grp[:].bitcast(F32).rearrange("p (w u) -> p w u", u=2),
+                    in_=banks[t][:].rearrange("p u w -> p w u"),
+                )
+            else:
+                nc.scalar.activation(
+                    out=grp[:].rearrange("p (w u e) -> p w u e", u=2, e=2),
+                    in_=banks[t][:].bitcast(BF16).rearrange("p u (w e) -> p w u e", e=2),
+                    func=SQUARE,
+                )
             return grp
 
         def quantise(t, grp):
@@ -114,7 +139,7 @@ def tile_custom_final_pooling_2d_kernel(tc, input_state, T_words, T_scales, out)
             for i in range(BUNCH):
                 t = BUNCH * j + i
                 codes, sc = quant[t]
-                acc = psum.tile([P, R], F32, name="acc%d" % t, tag="bank%d" % i)
+                acc = psum.tile([P, R], F32, name="acc%d" % t, tag="bank%d" % (BUNCH * (j % 2) + i))
                 for g in range(G):
                     nc.tensor.matmul_mx(
                         out=acc[:],
@@ -127,47 +152,33 @@ def tile_custom_final_pooling_2d_kernel(tc, input_state, T_words, T_scales, out)
                     )
                 accs[t] = acc
 
-        def empty(t, on_vector):
-            dst = stage[t // BUNCH][:, t % BUNCH, :]
-            if on_vector:
+        def empty(t):
+            n = store_size(t)
+            first = t - t % n
+            if t == first:
+                stage[first] = opool.tile([P, n, R], F32, name="ost%d" % first, tag="ost%d" % n)
+            dst = stage[first][:, t - first, :]
+            if empties_on_vector(t):
                 nc.vector.tensor_copy(out=dst, in_=accs[t][:])
             else:
                 nc.scalar.copy(out=dst, in_=accs[t][:])
+            if t == first + n - 1:
+                nc.sync.dma_start(out=ov[:, first : first + n, :], in_=stage[first][:])
 
-        square(0, 1)
-        square(1, 1)
-        square(2, 2)
-        for j in range(NB + 1):
-            a = BUNCH * j
-            o = a - BUNCH
-            if j < NB:
-                transposes(j)
-            if j >= 1:
-                multiply(j - 1)
-                stage[j - 1] = opool.tile([P, BUNCH, R], F32, name="ost%d" % (j - 1), tag="ost")
-            if j + 1 < NB:
-                square(a + 4, 2)
-            if j < NB:
-                quantise(a, regroup(a))
-                quantise(a + 1, regroup(a + 1))
-            if j + 1 < NB:
-                square(a + 6, 2)
-            if j < NB:
-                g2 = regroup(a + 2)
-                if j >= 1:
-                    empty(o, False)
-                quantise(a + 2, g2)
-                quantise(a + 3, regroup(a + 3))
-                if j >= 1:
-                    empty(o + 1, False)
-                    empty(o + 2, False)
-                    empty(o + 3, True)
-                    nc.sync.dma_start(out=ov[:, o : o + BUNCH, :], in_=stage[j - 1][:])
-            else:
-                empty(o, True)
-                empty(o + 1, False)
-                nc.sync.dma_start(out=ov[:, o : o + 2, :], in_=stage[j - 1][:, 0:2, :])
-                empty(o + 2, True)
-                nc.sync.dma_start(out=ov[:, o + 2 : o + 3, :], in_=stage[j - 1][:, 2:3, :])
-                empty(o + 3, False)
-                nc.sync.dma_start(out=ov[:, o + 3 : o + 4, :], in_=stage[j - 1][:, 3:4, :])
+        dummies(WARM)
+        for k in range(NB + LAG):
+            if k < NB:
+                transposes(k)
+                if k < 3:
+                    dummies(2)
+            if k >= LAG:
+                multiply(k - LAG)
+            for i in range(BUNCH):
+                ahead = BUNCH * (k + 2) + i
+                if ahead < TILES and is_sorted(ahead):
+                    square_sorted(ahead)
+                if k < NB:
+                    t = BUNCH * k + i
+                    quantise(t, regroup(t))
+                if k >= LAG:
+                    empty(BUNCH * (k - LAG) + i)

@@ -19,24 +19,24 @@ G = K // 512
 BUNCH = 2
 NB = TILES // BUNCH
 LAG = 2
-LOADS = [1, 1, 2, 4, 8, 8, 8]
-W_AFTER = 2
-WARM = 6
+LOADS = [1, 1, 2, 2, 2, 4, 4, 8, 8]
+W_AFTER = 4
+WARM = 4
 MULT = mybir.AluOpType.mult
 
 FLOPS = 2 * B * K * R
 
 
 def is_sorted(t):
-    return t >= 4 and t % 2 == 1
+    return t >= 30 or (t >= 4 and t % 2 == 1)
 
 
-def empties_on_vector(t):
-    return t % 8 in (0, 2, 3, 5, 6)
+def on_vector(t):
+    return t % 8 == 5
 
 
 def store_size(t):
-    return 4 if t < 24 else 2
+    return 4 if t < 24 else (2 if t < 28 else 1)
 
 
 def tile_custom_final_pooling_2d_kernel(tc, input_state, T_words, T_scales, out):
@@ -82,15 +82,14 @@ def tile_custom_final_pooling_2d_kernel(tc, input_state, T_words, T_scales, out)
 
         h_of = {}
         banks = {}
+        groups = {}
         quant = {}
         accs = {}
         stage = {}
 
         idle = psum.tile([P, 512], F32, name="idle", tag="bank7")
-
-        def dummies(n):
-            for d in range(n):
-                nc.tensor.matmul(out=idle[:], lhsT=zeros[:, 0:P], rhs=zeros[:], start=True, stop=True)
+        for d in range(WARM):
+            nc.tensor.matmul(out=idle[:], lhsT=zeros[:, 0:P], rhs=zeros[:], start=True, stop=True)
 
         def square_sorted(t):
             hs = hpool.tile([P, 2, 512], BF16, name="hs%d" % t, tag="hs")
@@ -100,57 +99,57 @@ def tile_custom_final_pooling_2d_kernel(tc, input_state, T_words, T_scales, out)
             )
             h_of[t] = hs
 
-        def transposes(j):
-            for i in range(BUNCH):
-                t = BUNCH * j + i
-                k = BUNCH * j + i if j < 2 else 4 + BUNCH * (j % 2) + i
-                bank = psum.tile([P, 2, 256], F32, name="xt%d" % t, tag="bank%d" % k)
-                for g in range(G):
-                    for u in range(2):
-                        if is_sorted(t):
-                            src = h_of[t][:, u, :].bitcast(F32)[:, P * g : P * (g + 1)]
-                        else:
-                            src = x_of[t].bitcast(F32)[:, 256 * g + u : 256 * (g + 1) : 2]
-                        nc.tensor.transpose(bank[:, u, P * g : P * (g + 1)], src, ident[:])
-                banks[t] = bank
+        def transposes(t):
+            j = t // BUNCH
+            k = t if j < 2 else 4 + BUNCH * (j % 2) + t % BUNCH
+            bank = psum.tile([P, 2, 256], F32, name="xt%d" % t, tag="bank%d" % k)
+            for g in range(G):
+                for u in range(2):
+                    if is_sorted(t):
+                        src = h_of[t][:, u, :].bitcast(F32)[:, P * g : P * (g + 1)]
+                    else:
+                        src = x_of[t].bitcast(F32)[:, 256 * g + u : 256 * (g + 1) : 2]
+                    nc.tensor.transpose(bank[:, u, P * g : P * (g + 1)], src, ident[:])
+            banks[t] = bank
 
         def regroup(t):
             grp = gpool.tile([P, K], BF16, name="grp%d" % t, tag="grp", align_bytes=64)
             if is_sorted(t):
-                nc.scalar.copy(
-                    out=grp[:].bitcast(F32).rearrange("p (w u) -> p w u", u=2),
-                    in_=banks[t][:].rearrange("p u w -> p w u"),
-                )
+                dst = grp[:].bitcast(F32).rearrange("p (w u) -> p w u", u=2)
+                src = banks[t][:].rearrange("p u w -> p w u")
+                if t % 2 == 1:
+                    nc.vector.tensor_copy(out=dst, in_=src)
+                else:
+                    nc.scalar.copy(out=dst, in_=src)
             else:
                 nc.scalar.activation(
                     out=grp[:].rearrange("p (w u e) -> p w u e", u=2, e=2),
                     in_=banks[t][:].bitcast(BF16).rearrange("p u (w e) -> p w u e", e=2),
                     func=SQUARE,
                 )
-            return grp
+            groups[t] = grp
 
-        def quantise(t, grp):
+        def quantise(t):
             codes = cpool.tile([P, K // 4], U32, name="codes%d" % t, tag="codes", align_bytes=64)
             sc = cpool.tile([P, K // 4], U8, name="sc%d" % t, tag="sc", align_bytes=64)
-            nc.vector.quantize_mx(out=codes[:].bitcast(FP8X4), scales=sc[:], in_=grp[:])
+            nc.vector.quantize_mx(out=codes[:].bitcast(FP8X4), scales=sc[:], in_=groups[t][:])
             quant[t] = (codes, sc)
 
-        def multiply(j):
-            for i in range(BUNCH):
-                t = BUNCH * j + i
-                codes, sc = quant[t]
-                acc = psum.tile([P, R], F32, name="acc%d" % t, tag="bank%d" % (BUNCH * (j % 2) + i))
-                for g in range(G):
-                    nc.tensor.matmul_mx(
-                        out=acc[:],
-                        lhsT=codes[:, P * g : P * (g + 1)].bitcast(FP8X4),
-                        lhsT_scale=sc[:, P * g : P * (g + 1)],
-                        rhs=w_words[:, g, :].bitcast(FP4X4),
-                        rhs_scale=w_sc[:, g, :],
-                        start=(g == 0),
-                        stop=(g == G - 1),
-                    )
-                accs[t] = acc
+        def multiply(t):
+            codes, sc = quant[t]
+            k = BUNCH * ((t // BUNCH) % 2) + t % BUNCH
+            acc = psum.tile([P, R], F32, name="acc%d" % t, tag="bank%d" % k)
+            for g in range(G):
+                nc.tensor.matmul_mx(
+                    out=acc[:],
+                    lhsT=codes[:, P * g : P * (g + 1)].bitcast(FP8X4),
+                    lhsT_scale=sc[:, P * g : P * (g + 1)],
+                    rhs=w_words[:, g, :].bitcast(FP4X4),
+                    rhs_scale=w_sc[:, g, :],
+                    start=(g == 0),
+                    stop=(g == G - 1),
+                )
+            accs[t] = acc
 
         def empty(t):
             n = store_size(t)
@@ -158,27 +157,27 @@ def tile_custom_final_pooling_2d_kernel(tc, input_state, T_words, T_scales, out)
             if t == first:
                 stage[first] = opool.tile([P, n, R], F32, name="ost%d" % first, tag="ost%d" % n)
             dst = stage[first][:, t - first, :]
-            if empties_on_vector(t):
+            if on_vector(t):
                 nc.vector.tensor_copy(out=dst, in_=accs[t][:])
             else:
                 nc.scalar.copy(out=dst, in_=accs[t][:])
             if t == first + n - 1:
                 nc.sync.dma_start(out=ov[:, first : first + n, :], in_=stage[first][:])
 
-        dummies(WARM)
         for k in range(NB + LAG):
-            if k < NB:
-                transposes(k)
-                if k < 3:
-                    dummies(2)
-            if k >= LAG:
-                multiply(k - LAG)
-            for i in range(BUNCH):
-                ahead = BUNCH * (k + 2) + i
-                if ahead < TILES and is_sorted(ahead):
-                    square_sorted(ahead)
-                if k < NB:
-                    t = BUNCH * k + i
-                    quantise(t, regroup(t))
-                if k >= LAG:
-                    empty(BUNCH * (k - LAG) + i)
+            new = [BUNCH * k + i for i in range(BUNCH) if k < NB]
+            old = [BUNCH * (k - LAG) + i for i in range(BUNCH) if k >= LAG]
+            ahead = [BUNCH * (k + 2) + i for i in range(BUNCH) if k + 2 < NB]
+            for t in new:
+                transposes(t)
+            for t in old:
+                multiply(t)
+            for t in new:
+                regroup(t)
+            for t in ahead:
+                if is_sorted(t):
+                    square_sorted(t)
+            for t in new:
+                quantise(t)
+            for t in old:
+                empty(t)

@@ -21,14 +21,17 @@ NB = TILES // BUNCH
 LAG = 2
 LOADS = [1, 1, 2, 2, 2, 4, 4, 8, 8]
 W_AFTER = 4
-WARM = 4
 MULT = mybir.AluOpType.mult
 
 FLOPS = 2 * B * K * R
 
 
 def is_sorted(t):
-    return t >= 30 or (t >= 4 and t % 2 == 1)
+    return t >= 28 or (t >= 6 and t % 2 == 1)
+
+
+def squared_by_vector(t):
+    return t in (1, 3)
 
 
 def on_vector(t):
@@ -36,7 +39,7 @@ def on_vector(t):
 
 
 def store_size(t):
-    return 4 if t < 24 else (2 if t < 28 else 1)
+    return 4 if t < 24 else 1
 
 
 def tile_custom_final_pooling_2d_kernel(tc, input_state, T_words, T_scales, out):
@@ -53,8 +56,6 @@ def tile_custom_final_pooling_2d_kernel(tc, input_state, T_words, T_scales, out)
         psum = ctx.enter_context(tc.psum_pool(name="psum", bufs=1))
         ctx.enter_context(tc.manual_schedule())
 
-        zeros = const.tile([P, 512], BF16, name="zeros")
-        nc.vector.memset(zeros[:], 0.0)
         w_sc = const.tile([P, G, R], U8, name="w_sc", align_bytes=64)
         nc.vector.memset(w_sc[:].bitcast(I32), 0)
         ident = const.tile([P, P], F32, name="ident")
@@ -87,10 +88,6 @@ def tile_custom_final_pooling_2d_kernel(tc, input_state, T_words, T_scales, out)
         accs = {}
         stage = {}
 
-        idle = psum.tile([P, 512], F32, name="idle", tag="bank7")
-        for d in range(WARM):
-            nc.tensor.matmul(out=idle[:], lhsT=zeros[:, 0:P], rhs=zeros[:], start=True, stop=True)
-
         def square_sorted(t):
             hs = hpool.tile([P, 2, 512], BF16, name="hs%d" % t, tag="hs")
             src = x_of[t].rearrange("p (w u e) -> p w u e", u=2, e=2)
@@ -114,13 +111,15 @@ def tile_custom_final_pooling_2d_kernel(tc, input_state, T_words, T_scales, out)
 
         def regroup(t):
             grp = gpool.tile([P, K], BF16, name="grp%d" % t, tag="grp", align_bytes=64)
-            if is_sorted(t):
+            if is_sorted(t) or squared_by_vector(t):
                 dst = grp[:].bitcast(F32).rearrange("p (w u) -> p w u", u=2)
                 src = banks[t][:].rearrange("p u w -> p w u")
                 if t % 2 == 1:
                     nc.vector.tensor_copy(out=dst, in_=src)
                 else:
                     nc.scalar.copy(out=dst, in_=src)
+                if squared_by_vector(t):
+                    nc.vector.tensor_tensor(out=grp[:], in0=grp[:], in1=grp[:], op=MULT)
             else:
                 nc.scalar.activation(
                     out=grp[:].rearrange("p (w u e) -> p w u e", u=2, e=2),
@@ -155,7 +154,9 @@ def tile_custom_final_pooling_2d_kernel(tc, input_state, T_words, T_scales, out)
             n = store_size(t)
             first = t - t % n
             if t == first:
-                stage[first] = opool.tile([P, n, R], F32, name="ost%d" % first, tag="ost%d" % n)
+                stage[first] = opool.tile(
+                    [P, n, R], F32, name="ost%d" % first, tag="ost%d" % n, bufs=(4 if n == 4 else 8)
+                )
             dst = stage[first][:, t - first, :]
             if on_vector(t):
                 nc.vector.tensor_copy(out=dst, in_=accs[t][:])

@@ -21,17 +21,14 @@ NB = TILES // BUNCH
 LAG = 2
 LOADS = [1, 1, 2, 2, 2, 4, 4, 8, 8]
 W_AFTER = 4
+WARM = 4
 MULT = mybir.AluOpType.mult
 
 FLOPS = 2 * B * K * R
 
 
 def is_sorted(t):
-    return t >= 28 or (t >= 6 and t % 2 == 1)
-
-
-def squared_by_vector(t):
-    return t in (1, 3)
+    return t >= 30 or (t >= 4 and t % 2 == 1)
 
 
 def on_vector(t):
@@ -39,7 +36,7 @@ def on_vector(t):
 
 
 def store_size(t):
-    return 4 if t < 24 else 1
+    return 4 if t < 24 else (2 if t < 26 else 1)
 
 
 def tile_custom_final_pooling_2d_kernel(tc, input_state, T_words, T_scales, out):
@@ -56,6 +53,8 @@ def tile_custom_final_pooling_2d_kernel(tc, input_state, T_words, T_scales, out)
         psum = ctx.enter_context(tc.psum_pool(name="psum", bufs=1))
         ctx.enter_context(tc.manual_schedule())
 
+        zeros = const.tile([P, 512], BF16, name="zeros")
+        nc.vector.memset(zeros[:], 0.0)
         w_sc = const.tile([P, G, R], U8, name="w_sc", align_bytes=64)
         nc.vector.memset(w_sc[:].bitcast(I32), 0)
         ident = const.tile([P, P], F32, name="ident")
@@ -88,6 +87,10 @@ def tile_custom_final_pooling_2d_kernel(tc, input_state, T_words, T_scales, out)
         accs = {}
         stage = {}
 
+        idle = psum.tile([P, 512], F32, name="idle", tag="bank7")
+        for d in range(WARM):
+            nc.tensor.matmul(out=idle[:], lhsT=zeros[:, 0:P], rhs=zeros[:], start=True, stop=True)
+
         def square_sorted(t):
             hs = hpool.tile([P, 2, 512], BF16, name="hs%d" % t, tag="hs")
             src = x_of[t].rearrange("p (w u e) -> p w u e", u=2, e=2)
@@ -111,15 +114,13 @@ def tile_custom_final_pooling_2d_kernel(tc, input_state, T_words, T_scales, out)
 
         def regroup(t):
             grp = gpool.tile([P, K], BF16, name="grp%d" % t, tag="grp", align_bytes=64)
-            if is_sorted(t) or squared_by_vector(t):
+            if is_sorted(t):
                 dst = grp[:].bitcast(F32).rearrange("p (w u) -> p w u", u=2)
                 src = banks[t][:].rearrange("p u w -> p w u")
                 if t % 2 == 1:
                     nc.vector.tensor_copy(out=dst, in_=src)
                 else:
                     nc.scalar.copy(out=dst, in_=src)
-                if squared_by_vector(t):
-                    nc.vector.tensor_tensor(out=grp[:], in0=grp[:], in1=grp[:], op=MULT)
             else:
                 nc.scalar.activation(
                     out=grp[:].rearrange("p (w u e) -> p w u e", u=2, e=2),
@@ -155,7 +156,7 @@ def tile_custom_final_pooling_2d_kernel(tc, input_state, T_words, T_scales, out)
             first = t - t % n
             if t == first:
                 stage[first] = opool.tile(
-                    [P, n, R], F32, name="ost%d" % first, tag="ost%d" % n, bufs=(4 if n == 4 else 8)
+                    [P, n, R], F32, name="ost%d" % first, tag="ost%d" % n, bufs=(6 if n == 1 else 4)
                 )
             dst = stage[first][:, t - first, :]
             if on_vector(t):

@@ -99,10 +99,15 @@ def tile_custom_final_pooling_2d_kernel(tc, input_state, T_words, T_scales, out)
             )
             h_of[t] = hs
 
+        def bridge(dst):
+            nc.tensor.matmul(out=dst, lhsT=zeros[:, 0:P], rhs=zeros[:, 0:32], start=True, stop=True)
+
         def transposes(t):
             j = t // BUNCH
             k = t if j < 2 else 4 + BUNCH * (j % 2) + t % BUNCH
             bank = psum.tile([P, 2, 256], F32, name="xt%d" % t, tag="bank%d" % k)
+            if t % BUNCH == 0 and j > LAG:
+                bridge(bank[:, 0, 0:32])
             for g in range(G):
                 for u in range(2):
                     if is_sorted(t):
@@ -139,6 +144,8 @@ def tile_custom_final_pooling_2d_kernel(tc, input_state, T_words, T_scales, out)
             codes, sc = quant[t]
             k = BUNCH * ((t // BUNCH) % 2) + t % BUNCH
             acc = psum.tile([P, R], F32, name="acc%d" % t, tag="bank%d" % k)
+            if t % BUNCH == 0 and t // BUNCH + LAG < NB:
+                bridge(acc[:, 0:32])
             for g in range(G):
                 nc.tensor.matmul_mx(
                     out=acc[:],

from contextlib import ExitStack

import concourse.mybir as mybir
from concourse.masks import make_identity

F32 = mybir.dt.float32
BF16 = mybir.dt.bfloat16
I32 = mybir.dt.int32
U32 = mybir.dt.uint32
U8 = mybir.dt.uint8
FP8X4 = mybir.dt.float8_e4m3fn_x4
FP4X4 = mybir.dt.float4_e2m1fn_x4
SQUARE = mybir.ActivationFunctionType.Square

P = 128
B, K, R = 4096, 1024, 512
TILES = B // P
G = K // 512
BUNCH = 2
NB = TILES // BUNCH
LAG = 2
LOADS = [1, 1, 2, 2, 2, 4, 4, 8, 8]
W_AFTER = 4
WARM = 4
MULT = mybir.AluOpType.mult

FLOPS = 2 * B * K * R


def is_sorted(t):
    return t >= 30 or (t >= 4 and t % 2 == 1)


def on_vector(t):
    return t % 8 == 5


def store_size(t):
    return 4 if t < 24 else (2 if t < 26 else 1)


def tile_custom_final_pooling_2d_kernel(tc, input_state, T_words, T_scales, out):
    nc = tc.nc
    xv = input_state.rearrange("(p j) k -> p j k", j=TILES)
    ov = out.rearrange("(p j) r -> p j r", j=TILES)
    with ExitStack() as ctx:
        const = ctx.enter_context(tc.tile_pool(name="const", bufs=1))
        xpool = ctx.enter_context(tc.tile_pool(name="xpool", bufs=1))
        hpool = ctx.enter_context(tc.tile_pool(name="hpool", bufs=6))
        gpool = ctx.enter_context(tc.tile_pool(name="gpool", bufs=6))
        cpool = ctx.enter_context(tc.tile_pool(name="cpool", bufs=12))
        opool = ctx.enter_context(tc.tile_pool(name="opool", bufs=4))
        psum = ctx.enter_context(tc.psum_pool(name="psum", bufs=1))
        ctx.enter_context(tc.manual_schedule())

        zeros = const.tile([P, 512], BF16, name="zeros")
        nc.vector.memset(zeros[:], 0.0)
        w_sc = const.tile([P, G, R], U8, name="w_sc", align_bytes=64)
        nc.vector.memset(w_sc[:].bitcast(I32), 0)
        ident = const.tile([P, P], F32, name="ident")
        make_identity(nc, ident[:])
        w_words = const.tile([P, G, 2 * R], U8, name="w_words", align_bytes=64)

        x_of = []
        j0 = 0
        for c, n in enumerate(LOADS):
            if c == W_AFTER:
                nc.sync.dma_start(
                    out=w_words[:].bitcast(I32),
                    in_=T_words.rearrange("g p b -> p g b").bitcast(I32),
                )
                for q in range(4):
                    nc.sync.dma_start(
                        out=w_sc[32 * q : 32 * q + 4, :, :].bitcast(I32),
                        in_=T_scales.rearrange("g q n -> q g n")[4 * q : 4 * q + 4].bitcast(I32),
                    )
            xc = xpool.tile([P, n, K], BF16, name="x%d" % c)
            nc.sync.dma_start(out=xc[:], in_=xv[:, j0 : j0 + n, :])
            for i in range(n):
                x_of.append(xc[:, i, :])
            j0 += n

        h_of = {}
        banks = {}
        groups = {}
        quant = {}
        accs = {}
        stage = {}

        idle = psum.tile([P, 512], F32, name="idle", tag="bank7")
        for d in range(WARM):
            nc.tensor.matmul(out=idle[:], lhsT=zeros[:, 0:P], rhs=zeros[:], start=True, stop=True)

        def square_sorted(t):
            hs = hpool.tile([P, 2, 512], BF16, name="hs%d" % t, tag="hs")
            src = x_of[t].rearrange("p (w u e) -> p w u e", u=2, e=2)
            nc.vector.tensor_tensor(
                out=hs[:].rearrange("p u (w e) -> p w u e", e=2), in0=src, in1=src, op=MULT
            )
            h_of[t] = hs

        def bridge(dst):
            nc.tensor.matmul(out=dst, lhsT=zeros[:, 0:P], rhs=zeros[:, 0:32], start=True, stop=True)

        def transposes(t):
            j = t // BUNCH
            k = t if j < 2 else 4 + BUNCH * (j % 2) + t % BUNCH
            bank = psum.tile([P, 2, 256], F32, name="xt%d" % t, tag="bank%d" % k)
            if t % BUNCH == 0 and j > LAG:
                bridge(bank[:, 0, 0:32])
            for g in range(G):
                for u in range(2):
                    if is_sorted(t):
                        src = h_of[t][:, u, :].bitcast(F32)[:, P * g : P * (g + 1)]
                    else:
                        src = x_of[t].bitcast(F32)[:, 256 * g + u : 256 * (g + 1) : 2]
                    nc.tensor.transpose(bank[:, u, P * g : P * (g + 1)], src, ident[:])
            banks[t] = bank

        def regroup(t):
            grp = gpool.tile([P, K], BF16, name="grp%d" % t, tag="grp", align_bytes=64)
            if is_sorted(t):
                dst = grp[:].bitcast(F32).rearrange("p (w u) -> p w u", u=2)
                src = banks[t][:].rearrange("p u w -> p w u")
                if t % 2 == 1:
                    nc.vector.tensor_copy(out=dst, in_=src)
                else:
                    nc.scalar.copy(out=dst, in_=src)
            else:
                nc.scalar.activation(
                    out=grp[:].rearrange("p (w u e) -> p w u e", u=2, e=2),
                    in_=banks[t][:].bitcast(BF16).rearrange("p u (w e) -> p w u e", e=2),
                    func=SQUARE,
                )
            groups[t] = grp

        def quantise(t):
            codes = cpool.tile([P, K // 4], U32, name="codes%d" % t, tag="codes", align_bytes=64)
            sc = cpool.tile([P, K // 4], U8, name="sc%d" % t, tag="sc", align_bytes=64)
            nc.vector.quantize_mx(out=codes[:].bitcast(FP8X4), scales=sc[:], in_=groups[t][:])
            quant[t] = (codes, sc)

        def multiply(t):
            codes, sc = quant[t]
            k = BUNCH * ((t // BUNCH) % 2) + t % BUNCH
            acc = psum.tile([P, R], F32, name="acc%d" % t, tag="bank%d" % k)
            if t % BUNCH == 0 and t // BUNCH + LAG < NB:
                bridge(acc[:, 0:32])
            for g in range(G):
                nc.tensor.matmul_mx(
                    out=acc[:],
                    lhsT=codes[:, P * g : P * (g + 1)].bitcast(FP8X4),
                    lhsT_scale=sc[:, P * g : P * (g + 1)],
                    rhs=w_words[:, g, :].bitcast(FP4X4),
                    rhs_scale=w_sc[:, g, :],
                    start=(g == 0),
                    stop=(g == G - 1),
                )
            accs[t] = acc

        def empty(t):
            n = store_size(t)
            first = t - t % n
            if t == first:
                stage[first] = opool.tile(
                    [P, n, R], F32, name="ost%d" % first, tag="ost%d" % n, bufs=(6 if n == 1 else 4)
                )
            dst = stage[first][:, t - first, :]
            if on_vector(t):
                nc.vector.tensor_copy(out=dst, in_=accs[t][:])
            else:
                nc.scalar.copy(out=dst, in_=accs[t][:])
            if t == first + n - 1:
                nc.sync.dma_start(out=ov[:, first : first + n, :], in_=stage[first][:])

        for k in range(NB + LAG):
            new = [BUNCH * k + i for i in range(BUNCH) if k < NB]
            old = [BUNCH * (k - LAG) + i for i in range(BUNCH) if k >= LAG]
            ahead = [BUNCH * (k + 2) + i for i in range(BUNCH) if k + 2 < NB]
            for t in new:
                transposes(t)
            for t in old:
                multiply(t)
            for t in new:
                regroup(t)
            for t in ahead:
                if is_sorted(t):
                    square_sorted(t)
            for t in new:
                quantise(t)
            for t in old:
                empty(t)
